import numpy as np
import ml_dtypes


BF16 = ml_dtypes.bfloat16


def bf(x):
    return np.asarray(x, np.float32).astype(BF16)


def f64(x):
    return np.asarray(x).astype(np.float64)


E2M1 = np.array([0.0, 0.5, 1.0, 1.5, 2.0, 3.0, 4.0, 6.0, -0.0, -0.5, -1.0, -1.5, -2.0, -3.0, -4.0, -6.0])


def pack_weight(w, fmt):
    k, n = w.shape
    w = f64(bf(w)).reshape(k // 32, 32, n)
    amax = np.abs(w).max(1)
    if fmt == "e4m3":
        byte = np.frexp(amax)[1] - 1 + 127 - 7
    else:
        mant, ex = np.frexp(amax / 6.0)
        byte = np.where(mant > 0.5, ex, ex - 1) + 127
    byte = np.clip(np.where(amax > 0, byte, 1), 1, 254)
    scaled = (w * np.exp2(127.0 - byte)[:, None, :]).reshape(k, n).astype(np.float32)
    by_word = np.ascontiguousarray(scaled.reshape(k // 512, 128, 4, n).transpose(0, 1, 3, 2))
    if fmt == "e4m3":
        words = by_word.astype(ml_dtypes.float8_e4m3fn).view(np.uint8)
    else:
        c = by_word.astype(ml_dtypes.float4_e2m1fn).view(np.uint8) & 0xF
        words = c[..., 0::2] | (c[..., 1::2] << 4)
    return np.ascontiguousarray(words), np.ascontiguousarray(byte.astype(np.uint8).reshape(k // 512, 16, n))


def unpack_weight(words, scales, fmt):
    g, p, n, _ = words.shape
    if fmt == "e4m3":
        vals = np.ascontiguousarray(words).view(ml_dtypes.float8_e4m3fn).astype(np.float64)
    else:
        nib = np.empty((g, p, n, 4), np.uint8)
        nib[..., 0::2] = words & 0xF
        nib[..., 1::2] = words >> 4
        vals = E2M1[nib]
    vals = vals * np.repeat(np.exp2(scales.astype(np.float64) - 127.0), 8, axis=1)[..., None]
    return vals.transpose(0, 1, 3, 2).reshape(g * 512, n)

def pack4(w):
    words, scales = pack_weight(w, "e2m1")
    return words.reshape(words.shape[0], 128, -1), scales


def unpack4(words, scales):
    return unpack_weight(words.reshape(words.shape[0], 128, -1, 2), scales, "e2m1")


def kspread(k):
    return np.exp2(np.repeat(np.random.randint(-6, 7, k // 32), 32).astype(np.float64))


B, T, D, H, KVH, HD = 2, 512, 2048, 16, 4, 128
HALF = HD // 2
EPS = 1e-6
ROPE_BASE = 10000.0


def zc_rmsnorm(x, scale):
    rms = np.sqrt(np.mean(x ** 2, axis=-1, keepdims=True) + EPS)
    return (1.0 + scale) * x / rms


def apply_rope(x, cos, sin):
    t = x.shape[2]
    c = cos[:t][None, None, :, :]
    s = sin[:t][None, None, :, :]
    x1, x2 = x[..., :HALF], x[..., HALF:]
    return np.concatenate([x1 * c - x2 * s, x2 * c + x1 * s], axis=-1)


def setup_inputs():
    s = kspread(D)
    inv_freq = 1.0 / (ROPE_BASE ** (np.arange(0, HALF) / HALF))
    ang = np.arange(T)[:, None] * inv_freq[None, :]
    q_input = np.random.standard_normal((B, T, D)) * s
    q_input_words, q_input_scales = pack4(q_input.reshape(B * T, D).T)
    words, scales = pack4(np.random.standard_normal((D, H * HD)) / np.sqrt(D) / s[:, None])
    return {"q_input_words": q_input_words, "q_input_scales": q_input_scales,
            "Wq_words": words, "Wq_scales": scales,
            "q_scale": bf(np.random.standard_normal(HD) * 0.2),
            "cos": bf(np.cos(ang)), "sin": bf(np.sin(ang))}


def reference(q_input_words, q_input_scales, Wq_words, Wq_scales, q_scale, cos, sin):
    b = B
    q = unpack4(q_input_words, q_input_scales).T.reshape(B, T, D) @ unpack4(Wq_words, Wq_scales)
    q = q.reshape(b, -1, H, HD).transpose(0, 2, 1, 3)
    q = zc_rmsnorm(q, f64(q_scale))
    return apply_rope(q, f64(cos), f64(sin))

@@ -1,0 +1,164 @@
+from contextlib import ExitStack
+
+import concourse.mybir as mybir
+
+FLOPS = 2 * 1024 * 2048 * 2048
+
+F32 = mybir.dt.float32
+BF16 = mybir.dt.bfloat16
+U8 = mybir.dt.uint8
+I32 = mybir.dt.int32
+FP4X4 = mybir.dt.float4_e2m1fn_x4
+ALU = mybir.AluOpType
+ACT = mybir.ActivationFunctionType
+
+P = 128
+PASSES = 4
+HEAD = 128
+HALF = 64
+N_TILE = 512
+BANK_HEADS = 4
+POS_TILES = 4
+BATCHES = 2
+COL_BLOCKS = 4
+EPS = 1e-6
+WARM = 6
+
+
+def tile_multiheadattention_pa_kernel(
+    tc, q_input_words, q_input_scales, Wq_words, Wq_scales, q_scale, cos, sin, out
+):
+    nc = tc.nc
+    with ExitStack() as ctx:
+        const = ctx.enter_context(tc.tile_pool(name="const", bufs=1))
+        work = ctx.enter_context(tc.tile_pool(name="work", bufs=4))
+        small = ctx.enter_context(tc.tile_pool(name="small", bufs=6))
+        psum = ctx.enter_context(tc.psum_pool(name="psum", bufs=8))
+        ctx.enter_context(tc.manual_schedule())
+
+        x_codes = [const.tile([P, PASSES, 1024], U8, name="x_codes%d" % b, align_bytes=64) for b in range(BATCHES)]
+        x_planes = [const.tile([P, PASSES, 512], U8, name="x_planes%d" % b, align_bytes=64) for b in range(BATCHES)]
+        w_codes = [const.tile([P, PASSES, 1024], U8, name="w_codes%d" % n, align_bytes=64) for n in range(COL_BLOCKS)]
+        w_planes = [const.tile([P, PASSES, 512], U8, name="w_planes%d" % n, align_bytes=64) for n in range(COL_BLOCKS)]
+
+        def load_codes(dst, src, block):
+            nc.sync.dma_start(
+                out=dst[:].bitcast(I32),
+                in_=src[:, :, 1024 * block : 1024 * (block + 1)].rearrange("g p c -> p g c").bitcast(I32),
+            )
+
+        def load_planes(dst, src, block):
+            for quad in range(4):
+                nc.sync.dma_start(
+                    out=dst[32 * quad : 32 * quad + 4, :, :].bitcast(I32),
+                    in_=src[:, 4 * quad : 4 * quad + 4, 512 * block : 512 * (block + 1)]
+                    .rearrange("g r c -> r g c")
+                    .bitcast(I32),
+                )
+
+        eps = const.tile([P, 1], F32, name="eps")
+        nc.vector.memset(x_planes[0][:].bitcast(I32), 0)
+        nc.vector.memset(w_planes[0][:].bitcast(I32), 0)
+        nc.vector.memset(eps[:], EPS)
+        nc.vector.memset(x_planes[1][:].bitcast(I32), 0)
+        for n in range(1, COL_BLOCKS):
+            nc.vector.memset(w_planes[n][:].bitcast(I32), 0)
+
+        gain_rows = const.tile([P, 256], BF16, name="gain_rows")
+        ones = const.tile([P, N_TILE], BF16, name="ones")
+        nc.gpsimd.memset(gain_rows[:], 0.0)
+        nc.gpsimd.memset(ones[:], 1.0)
+
+        load_codes(x_codes[0], q_input_words, 0)
+        load_codes(w_codes[0], Wq_words, 0)
+        load_planes(x_planes[0], q_input_scales, 0)
+        load_planes(w_planes[0], Wq_scales, 0)
+        load_codes(x_codes[1], q_input_words, 1)
+        load_planes(x_planes[1], q_input_scales, 1)
+        for n in range(1, COL_BLOCKS):
+            load_codes(w_codes[n], Wq_words, n)
+            load_planes(w_planes[n], Wq_scales, n)
+
+        cos_sb = const.tile([P, POS_TILES, HALF], BF16, name="cos_sb")
+        sin_sb = const.tile([P, POS_TILES, HALF], BF16, name="sin_sb")
+        nc.scalar.dma_start(out=cos_sb[:], in_=cos.rearrange("(t p) j -> p t j", p=P))
+        nc.scalar.dma_start(out=sin_sb[:], in_=sin.rearrange("(t p) j -> p t j", p=P))
+        nc.scalar.dma_start(out=gain_rows[0:1, 0:HEAD], in_=q_scale.unsqueeze(0))
+        warm_act = const.tile([P, 1], F32, name="warm_act")
+        nc.scalar.activation(out=warm_act[:], in_=eps[:], func=ACT.Abs_reciprocal_sqrt)
+
+        warm_ps = psum.tile([P, N_TILE], F32, tag="acc", name="warm_ps")
+        for i in range(WARM // 2):
+            nc.tensor.matmul(out=warm_ps[:], lhsT=ones[:, 0:P], rhs=ones[:], start=True, stop=True)
+        gain_ps = psum.tile([P, N_TILE], F32, tag="acc", name="gain_ps")
+        nc.tensor.matmul(out=gain_ps[:, 0:256], lhsT=ones[:, 0:P], rhs=gain_rows[:], start=True, stop=True)
+        for i in range(WARM - WARM // 2):
+            nc.tensor.matmul(out=warm_ps[:], lhsT=ones[:, 0:P], rhs=ones[:], start=True, stop=True)
+
+        gain = const.tile([P, 2, HALF], F32, name="gain")
+        gain_sw = const.tile([P, 2, HALF], F32, name="gain_sw")
+        tab_a = const.tile([P, POS_TILES, 2, HALF], F32, name="tab_a")
+        tab_b = const.tile([P, POS_TILES, 2, HALF], F32, name="tab_b")
+        nc.vector.tensor_scalar_add(
+            out=gain[:].rearrange("p two j -> p (two j)"), in0=gain_ps[:, 0:HEAD], scalar1=1.0
+        )
+        nc.vector.tensor_scalar(
+            out=gain_sw[:, 0, :], in0=gain_ps[:, HALF:HEAD], scalar1=-1.0, scalar2=-1.0, op0=ALU.mult, op1=ALU.add
+        )
+        nc.vector.tensor_scalar_add(out=gain_sw[:, 1, :], in0=gain_ps[:, 0:HALF], scalar1=1.0)
+        full = [P, POS_TILES, 2, HALF]
+        nc.vector.tensor_tensor(
+            out=tab_a[:], in0=cos_sb[:].unsqueeze(2).to_broadcast(full), in1=gain[:].unsqueeze(1).to_broadcast(full), op=ALU.mult
+        )
+        nc.vector.tensor_tensor(
+            out=tab_b[:], in0=sin_sb[:].unsqueeze(2).to_broadcast(full), in1=gain_sw[:].unsqueeze(1).to_broadcast(full), op=ALU.mult
+        )
+
+        for n in range(COL_BLOCKS):
+            for m in range(BATCHES * POS_TILES):
+                b, pt = divmod(m, POS_TILES)
+                acc = psum.tile([P, N_TILE], F32, tag="acc", name="acc")
+                for g in range(PASSES):
+                    nc.tensor.matmul_mx(
+                        out=acc[:],
+                        lhsT=x_codes[b][:, g, 256 * pt : 256 * (pt + 1)].bitcast(FP4X4),
+                        lhsT_scale=x_planes[b][:, g, P * pt : P * (pt + 1)],
+                        rhs=w_codes[n][:, g, :].bitcast(FP4X4),
+                        rhs_scale=w_planes[n][:, g, :],
+                        start=(g == 0),
+                        stop=(g == PASSES - 1),
+                    )
+                ss = small.tile([P, BANK_HEADS], F32, name="ss")
+                rstd = small.tile([P, BANK_HEADS], F32, name="rstd")
+                for h in range(BANK_HEADS):
+                    junk = work.tile([P, HEAD], F32, name="junk")
+                    nc.scalar.activation(
+                        out=junk[:], in_=acc[:, HEAD * h : HEAD * (h + 1)], func=ACT.Square, accum_out=ss[:, h : h + 1]
+                    )
+                nc.scalar.activation(
+                    out=rstd[:], in_=ss[:], func=ACT.Abs_reciprocal_sqrt, scale=1.0 / HEAD, bias=eps[:, 0:1]
+                )
+                halves = acc[:].rearrange("p (h two j) -> p h two j", two=2, j=HALF)
+                t1 = work.tile([P, BANK_HEADS, 2, HALF], F32, name="t1")
+                t2 = work.tile([P, BANK_HEADS, 2, HALF], F32, name="t2")
+                for h in range(BANK_HEADS):
+                    nc.vector.scalar_tensor_tensor(
+                        out=t1[:, h, :, :], in0=halves[:, h, :, :], scalar=rstd[:, h : h + 1], in1=tab_a[:, pt, :, :],
+                        op0=ALU.mult, op1=ALU.mult,
+                    )
+                for h in range(BANK_HEADS):
+                    nc.vector.scalar_tensor_tensor(
+                        out=t2[:, h, :, :], in0=halves[:, h, ::-1, :], scalar=rstd[:, h : h + 1], in1=tab_b[:, pt, :, :],
+                        op0=ALU.mult, op1=ALU.mult,
+                    )
+                res = work.tile([P, BANK_HEADS, HEAD], F32, name="res")
+                nc.gpsimd.tensor_tensor(
+                    out=res[:].rearrange("p h d -> p (h d)"),
+                    in0=t1[:].rearrange("p h two j -> p (h two j)"),
+                    in1=t2[:].rearrange("p h two j -> p (h two j)"),
+                    op=ALU.add,
+                )
+                nc.sync.dma_start(
+                    out=out[b, BANK_HEADS * n : BANK_HEADS * (n + 1), P * pt : P * (pt + 1), :].rearrange("h p d -> p h d"),
+                    in_=res[:],
+                )

@@ -19,10 +19,39 @@ HALF = 64
 N_TILE = 512
 BANK_HEADS = 4
 POS_TILES = 4
-BATCHES = 2
+TOKEN_TILES = 8
 COL_BLOCKS = 4
 EPS = 1e-6
-WARM = 6
+WARM_A = 8
+WARM_B = 6
+GROUP_HEADS = 8
+V_GROUPS = 4
+W_CHUNKS = [(0, 1), (1, 4)]
+X_CHUNKS = [(0, 2), (2, 8)]
+
+
+def make_groups():
+    banks = [(n, m) for n in range(COL_BLOCKS) for m in range(TOKEN_TILES)]
+    groups = []
+    n, m = banks[0]
+    for h0, nh in [(0, 1), (1, 1), (2, 2)]:
+        groups.append([(n, m, h0, nh)])
+    middle = banks[1:-1]
+    lead = 1
+    for n, m in middle[:lead]:
+        groups.append([(n, m, 0, BANK_HEADS)])
+    per = GROUP_HEADS // BANK_HEADS
+    rest = middle[lead:]
+    trail = len(rest) % per + 0
+    body = rest[: len(rest) - trail]
+    for i in range(0, len(body), per):
+        groups.append([(n, m, 0, BANK_HEADS) for n, m in body[i : i + per]])
+    for n, m in rest[len(rest) - trail :]:
+        groups.append([(n, m, 0, BANK_HEADS)])
+    n, m = banks[-1]
+    for h0, nh in [(0, 2), (2, 1), (3, 1)]:
+        groups.append([(n, m, h0, nh)])
+    return groups
 
 
 def tile_multiheadattention_pa_kernel(
@@ -31,134 +60,187 @@ def tile_multiheadattention_pa_kernel(
     nc = tc.nc
     with ExitStack() as ctx:
         const = ctx.enter_context(tc.tile_pool(name="const", bufs=1))
-        work = ctx.enter_context(tc.tile_pool(name="work", bufs=4))
-        small = ctx.enter_context(tc.tile_pool(name="small", bufs=6))
+        work = ctx.enter_context(tc.tile_pool(name="work", bufs=5))
+        small = ctx.enter_context(tc.tile_pool(name="small", bufs=8))
         psum = ctx.enter_context(tc.psum_pool(name="psum", bufs=8))
         ctx.enter_context(tc.manual_schedule())
 
-        x_codes = [const.tile([P, PASSES, 1024], U8, name="x_codes%d" % b, align_bytes=64) for b in range(BATCHES)]
-        x_planes = [const.tile([P, PASSES, 512], U8, name="x_planes%d" % b, align_bytes=64) for b in range(BATCHES)]
-        w_codes = [const.tile([P, PASSES, 1024], U8, name="w_codes%d" % n, align_bytes=64) for n in range(COL_BLOCKS)]
-        w_planes = [const.tile([P, PASSES, 512], U8, name="w_planes%d" % n, align_bytes=64) for n in range(COL_BLOCKS)]
+        x_codes = [
+            const.tile([P, PASSES, 256 * (m1 - m0)], U8, name="x_codes%d" % m0, align_bytes=64) for m0, m1 in X_CHUNKS
+        ]
+        x_planes = [
+            const.tile([P, PASSES, P * (m1 - m0)], U8, name="x_planes%d" % m0, align_bytes=64) for m0, m1 in X_CHUNKS
+        ]
+        w_codes = [
+            const.tile([P, PASSES, 2 * N_TILE * (n1 - n0)], U8, name="w_codes%d" % n0, align_bytes=64) for n0, n1 in W_CHUNKS
+        ]
+        w_planes = [
+            const.tile([P, PASSES, N_TILE * (n1 - n0)], U8, name="w_planes%d" % n0, align_bytes=64) for n0, n1 in W_CHUNKS
+        ]
 
-        def load_codes(dst, src, block):
+        def load_codes(dst, src, c0, c1):
             nc.sync.dma_start(
-                out=dst[:].bitcast(I32),
-                in_=src[:, :, 1024 * block : 1024 * (block + 1)].rearrange("g p c -> p g c").bitcast(I32),
+                out=dst[:].bitcast(I32), in_=src[:, :, 2 * c0 : 2 * c1].rearrange("g p c -> p g c").bitcast(I32)
             )
 
-        def load_planes(dst, src, block):
+        def load_planes(dst, src, c0, c1):
             for quad in range(4):
                 nc.sync.dma_start(
                     out=dst[32 * quad : 32 * quad + 4, :, :].bitcast(I32),
-                    in_=src[:, 4 * quad : 4 * quad + 4, 512 * block : 512 * (block + 1)]
-                    .rearrange("g r c -> r g c")
-                    .bitcast(I32),
+                    in_=src[:, 4 * quad : 4 * quad + 4, c0:c1].rearrange("g r c -> r g c").bitcast(I32),
                 )
 
         eps = const.tile([P, 1], F32, name="eps")
         nc.vector.memset(x_planes[0][:].bitcast(I32), 0)
         nc.vector.memset(w_planes[0][:].bitcast(I32), 0)
         nc.vector.memset(eps[:], EPS)
-        nc.vector.memset(x_planes[1][:].bitcast(I32), 0)
-        for n in range(1, COL_BLOCKS):
-            nc.vector.memset(w_planes[n][:].bitcast(I32), 0)
+        for i in range(1, len(X_CHUNKS)):
+            nc.vector.memset(x_planes[i][:].bitcast(I32), 0)
+        for i in range(1, len(W_CHUNKS)):
+            nc.vector.memset(w_planes[i][:].bitcast(I32), 0)
 
         gain_rows = const.tile([P, 256], BF16, name="gain_rows")
-        ones = const.tile([P, N_TILE], BF16, name="ones")
-        nc.gpsimd.memset(gain_rows[:], 0.0)
-        nc.gpsimd.memset(ones[:], 1.0)
-
-        load_codes(x_codes[0], q_input_words, 0)
-        load_codes(w_codes[0], Wq_words, 0)
-        load_planes(x_planes[0], q_input_scales, 0)
-        load_planes(w_planes[0], Wq_scales, 0)
-        load_codes(x_codes[1], q_input_words, 1)
-        load_planes(x_planes[1], q_input_scales, 1)
-        for n in range(1, COL_BLOCKS):
-            load_codes(w_codes[n], Wq_words, n)
-            load_planes(w_planes[n], Wq_scales, n)
-
+        ones = const.tile([P, 256], BF16, name="ones")
         cos_sb = const.tile([P, POS_TILES, HALF], BF16, name="cos_sb")
         sin_sb = const.tile([P, POS_TILES, HALF], BF16, name="sin_sb")
-        nc.scalar.dma_start(out=cos_sb[:], in_=cos.rearrange("(t p) j -> p t j", p=P))
-        nc.scalar.dma_start(out=sin_sb[:], in_=sin.rearrange("(t p) j -> p t j", p=P))
-        nc.scalar.dma_start(out=gain_rows[0:1, 0:HEAD], in_=q_scale.unsqueeze(0))
+        nc.gpsimd.memset(ones[:], 1.0)
+        nc.gpsimd.memset(gain_rows[:], 0.0)
+        nc.gpsimd.dma_start(out=gain_rows[0:1, 0:HEAD], in_=q_scale.unsqueeze(0))
+        nc.gpsimd.dma_start(out=cos_sb[:], in_=cos.rearrange("(t p) j -> p t j", p=P))
+        nc.gpsimd.dma_start(out=sin_sb[:], in_=sin.rearrange("(t p) j -> p t j", p=P))
+
+        def load_x(i, what):
+            m0, m1 = X_CHUNKS[i]
+            if what == "codes":
+                load_codes(x_codes[i], q_input_words, P * m0, P * m1)
+            else:
+                load_planes(x_planes[i], q_input_scales, P * m0, P * m1)
+
+        def load_w(i, what):
+            n0, n1 = W_CHUNKS[i]
+            if what == "codes":
+                load_codes(w_codes[i], Wq_words, N_TILE * n0, N_TILE * n1)
+            else:
+                load_planes(w_planes[i], Wq_scales, N_TILE * n0, N_TILE * n1)
+
+        load_x(0, "codes")
+        load_w(0, "codes")
+        load_x(0, "planes")
+        load_w(0, "planes")
+        for i in range(1, len(X_CHUNKS)):
+            load_x(i, "planes")
+            load_x(i, "codes")
+        for i in range(1, len(W_CHUNKS)):
+            load_w(i, "planes")
+            load_w(i, "codes")
+
         warm_act = const.tile([P, 1], F32, name="warm_act")
         nc.scalar.activation(out=warm_act[:], in_=eps[:], func=ACT.Abs_reciprocal_sqrt)
 
         warm_ps = psum.tile([P, N_TILE], F32, tag="acc", name="warm_ps")
-        for i in range(WARM // 2):
-            nc.tensor.matmul(out=warm_ps[:], lhsT=ones[:, 0:P], rhs=ones[:], start=True, stop=True)
+        for i in range(WARM_A):
+            nc.tensor.matmul(out=warm_ps[:, 0:256], lhsT=ones[:, 0:P], rhs=ones[:], start=True, stop=True)
         gain_ps = psum.tile([P, N_TILE], F32, tag="acc", name="gain_ps")
         nc.tensor.matmul(out=gain_ps[:, 0:256], lhsT=ones[:, 0:P], rhs=gain_rows[:], start=True, stop=True)
-        for i in range(WARM - WARM // 2):
-            nc.tensor.matmul(out=warm_ps[:], lhsT=ones[:, 0:P], rhs=ones[:], start=True, stop=True)
+        for i in range(WARM_B):
+            nc.tensor.matmul(out=warm_ps[:, 0:256], lhsT=ones[:, 0:P], rhs=ones[:], start=True, stop=True)
 
         gain = const.tile([P, 2, HALF], F32, name="gain")
-        gain_sw = const.tile([P, 2, HALF], F32, name="gain_sw")
-        tab_a = const.tile([P, POS_TILES, 2, HALF], F32, name="tab_a")
-        tab_b = const.tile([P, POS_TILES, 2, HALF], F32, name="tab_b")
+        gain_pm = const.tile([P, 2, HALF], F32, name="gain_pm")
+        table = const.tile([P, POS_TILES, 2, 2, HALF], F32, name="table")
         nc.vector.tensor_scalar_add(
             out=gain[:].rearrange("p two j -> p (two j)"), in0=gain_ps[:, 0:HEAD], scalar1=1.0
         )
+        nc.vector.tensor_scalar_add(out=gain_pm[:, 0, :], in0=gain_ps[:, 0:HALF], scalar1=1.0)
         nc.vector.tensor_scalar(
-            out=gain_sw[:, 0, :], in0=gain_ps[:, HALF:HEAD], scalar1=-1.0, scalar2=-1.0, op0=ALU.mult, op1=ALU.add
+            out=gain_pm[:, 1, :], in0=gain_ps[:, HALF:HEAD], scalar1=-1.0, scalar2=-1.0, op0=ALU.mult, op1=ALU.add
         )
-        nc.vector.tensor_scalar_add(out=gain_sw[:, 1, :], in0=gain_ps[:, 0:HALF], scalar1=1.0)
         full = [P, POS_TILES, 2, HALF]
         nc.vector.tensor_tensor(
-            out=tab_a[:], in0=cos_sb[:].unsqueeze(2).to_broadcast(full), in1=gain[:].unsqueeze(1).to_broadcast(full), op=ALU.mult
+            out=table[:, :, 0, :, :], in0=cos_sb[:].unsqueeze(2).to_broadcast(full), in1=gain[:].unsqueeze(1).to_broadcast(full), op=ALU.mult
         )
         nc.vector.tensor_tensor(
-            out=tab_b[:], in0=sin_sb[:].unsqueeze(2).to_broadcast(full), in1=gain_sw[:].unsqueeze(1).to_broadcast(full), op=ALU.mult
+            out=table[:, :, 1, :, :], in0=sin_sb[:].unsqueeze(2).to_broadcast(full), in1=gain_pm[:].unsqueeze(1).to_broadcast(full), op=ALU.mult
         )
 
-        for n in range(COL_BLOCKS):
-            for m in range(BATCHES * POS_TILES):
+        def x_operand(m, g):
+            for i, (m0, m1) in enumerate(X_CHUNKS):
+                if m0 <= m < m1:
+                    k = m - m0
+                    return x_codes[i][:, g, 256 * k : 256 * (k + 1)], x_planes[i][:, g, P * k : P * (k + 1)]
+            raise ValueError("no chunk")
+
+        def w_operand(n, g, h0, nh):
+            for i, (n0, n1) in enumerate(W_CHUNKS):
+                if n0 <= n < n1:
+                    c0 = N_TILE * (n - n0) + HEAD * h0
+                    c1 = c0 + HEAD * nh
+                    return w_codes[i][:, g, 2 * c0 : 2 * c1], w_planes[i][:, g, c0:c1]
+            raise ValueError("no chunk")
+
+        def add_and_store(engine, group, prod, res):
+            off = sum(nh for n, m, h0, nh in group)
+            engine.tensor_tensor(
+                out=res[:, 0:off, :].rearrange("p h (two j) -> p h two j", two=2),
+                in0=prod[:, 0:off, 0, :, :],
+                in1=prod[:, 0:off, 1, ::-1, :],
+                op=ALU.add,
+            )
+            off = 0
+            for n, m, h0, nh in group:
                 b, pt = divmod(m, POS_TILES)
+                head0 = BANK_HEADS * n + h0
+                nc.sync.dma_start(
+                    out=out[b, head0 : head0 + nh, P * pt : P * (pt + 1), :].rearrange("h p d -> p h d"),
+                    in_=res[:, off : off + nh, :],
+                )
+                off += nh
+
+        groups = make_groups()
+        late = []
+        for gi, group in enumerate(groups):
+            prod = work.tile([P, GROUP_HEADS, 2, 2, HALF], F32, name="prod")
+            res = work.tile([P, GROUP_HEADS, HEAD], F32, name="res")
+            off = 0
+            for n, m, h0, nh in group:
+                pt = m % POS_TILES
+                width = HEAD * nh
                 acc = psum.tile([P, N_TILE], F32, tag="acc", name="acc")
                 for g in range(PASSES):
+                    xc, xp = x_operand(m, g)
+                    wc, wp = w_operand(n, g, h0, nh)
                     nc.tensor.matmul_mx(
-                        out=acc[:],
-                        lhsT=x_codes[b][:, g, 256 * pt : 256 * (pt + 1)].bitcast(FP4X4),
-                        lhsT_scale=x_planes[b][:, g, P * pt : P * (pt + 1)],
-                        rhs=w_codes[n][:, g, :].bitcast(FP4X4),
-                        rhs_scale=w_planes[n][:, g, :],
+                        out=acc[:, 0:width],
+                        lhsT=xc.bitcast(FP4X4),
+                        lhsT_scale=xp,
+                        rhs=wc.bitcast(FP4X4),
+                        rhs_scale=wp,
                         start=(g == 0),
                         stop=(g == PASSES - 1),
                     )
                 ss = small.tile([P, BANK_HEADS], F32, name="ss")
                 rstd = small.tile([P, BANK_HEADS], F32, name="rstd")
-                for h in range(BANK_HEADS):
-                    junk = work.tile([P, HEAD], F32, name="junk")
+                for h in range(nh):
+                    junk = small.tile([P, HEAD], F32, name="junk")
                     nc.scalar.activation(
                         out=junk[:], in_=acc[:, HEAD * h : HEAD * (h + 1)], func=ACT.Square, accum_out=ss[:, h : h + 1]
                     )
                 nc.scalar.activation(
-                    out=rstd[:], in_=ss[:], func=ACT.Abs_reciprocal_sqrt, scale=1.0 / HEAD, bias=eps[:, 0:1]
+                    out=rstd[:, 0:nh], in_=ss[:, 0:nh], func=ACT.Abs_reciprocal_sqrt, scale=1.0 / HEAD, bias=eps[:, 0:1]
                 )
-                halves = acc[:].rearrange("p (h two j) -> p h two j", two=2, j=HALF)
-                t1 = work.tile([P, BANK_HEADS, 2, HALF], F32, name="t1")
-                t2 = work.tile([P, BANK_HEADS, 2, HALF], F32, name="t2")
-                for h in range(BANK_HEADS):
+                for h in range(nh):
                     nc.vector.scalar_tensor_tensor(
-                        out=t1[:, h, :, :], in0=halves[:, h, :, :], scalar=rstd[:, h : h + 1], in1=tab_a[:, pt, :, :],
-                        op0=ALU.mult, op1=ALU.mult,
+                        out=prod[:, off + h, :, :, :].rearrange("p e two j -> p e (two j)"),
+                        in0=acc[:, HEAD * h : HEAD * (h + 1)].unsqueeze(1).to_broadcast([P, 2, HEAD]),
+                        scalar=rstd[:, h : h + 1],
+                        in1=table[:, pt, :, :, :].rearrange("p e two j -> p e (two j)"),
+                        op0=ALU.mult,
+                        op1=ALU.mult,
                     )
-                for h in range(BANK_HEADS):
-                    nc.vector.scalar_tensor_tensor(
-                        out=t2[:, h, :, :], in0=halves[:, h, ::-1, :], scalar=rstd[:, h : h + 1], in1=tab_b[:, pt, :, :],
-                        op0=ALU.mult, op1=ALU.mult,
-                    )
-                res = work.tile([P, BANK_HEADS, HEAD], F32, name="res")
-                nc.gpsimd.tensor_tensor(
-                    out=res[:].rearrange("p h d -> p (h d)"),
-                    in0=t1[:].rearrange("p h two j -> p (h two j)"),
-                    in1=t2[:].rearrange("p h two j -> p (h two j)"),
-                    op=ALU.add,
-                )
-                nc.sync.dma_start(
-                    out=out[b, BANK_HEADS * n : BANK_HEADS * (n + 1), P * pt : P * (pt + 1), :].rearrange("h p d -> p h d"),
-                    in_=res[:],
-                )
+                off += nh
+            if gi < len(groups) - V_GROUPS:
+                add_and_store(nc.gpsimd, group, prod, res)
+            else:
+                late.append((group, prod, res))
+        for group, prod, res in late:
+            add_and_store(nc.vector, group, prod, res)

@@ -22,34 +22,32 @@ POS_TILES = 4
 TOKEN_TILES = 8
 COL_BLOCKS = 4
 EPS = 1e-6
-WARM_A = 8
-WARM_B = 6
-GROUP_HEADS = 8
-V_GROUPS = 4
+WARM_A = 2
+WARM_B = 14
+GROUP_HEADS = 12
+V_GROUPS = 5
 W_CHUNKS = [(0, 1), (1, 4)]
 X_CHUNKS = [(0, 2), (2, 8)]
+HEAD_SPLIT = [(0, 1), (1, 1), (2, 2)]
+TAIL_SPLIT = [(0, 2), (2, 1), (3, 1)]
+MIDDLE_SIZES = [1, 2, 3, 3, 3, 3, 3, 3, 3, 2, 2, 1, 1]
+LAG_SQUARES = 2
+STORE_BY_HEAD = False
 
 
 def make_groups():
     banks = [(n, m) for n in range(COL_BLOCKS) for m in range(TOKEN_TILES)]
     groups = []
     n, m = banks[0]
-    for h0, nh in [(0, 1), (1, 1), (2, 2)]:
+    for h0, nh in HEAD_SPLIT:
         groups.append([(n, m, h0, nh)])
-    middle = banks[1:-1]
-    lead = 1
-    for n, m in middle[:lead]:
-        groups.append([(n, m, 0, BANK_HEADS)])
-    per = GROUP_HEADS // BANK_HEADS
-    rest = middle[lead:]
-    trail = len(rest) % per + 0
-    body = rest[: len(rest) - trail]
-    for i in range(0, len(body), per):
-        groups.append([(n, m, 0, BANK_HEADS) for n, m in body[i : i + per]])
-    for n, m in rest[len(rest) - trail :]:
-        groups.append([(n, m, 0, BANK_HEADS)])
+    at = 1
+    for size in MIDDLE_SIZES:
+        groups.append([(n, m, 0, BANK_HEADS) for n, m in banks[at : at + size]])
+        at += size
+    assert at == len(banks) - 1
     n, m = banks[-1]
-    for h0, nh in [(0, 2), (2, 1), (3, 1)]:
+    for h0, nh in TAIL_SPLIT:
         groups.append([(n, m, h0, nh)])
     return groups
 
@@ -60,7 +58,7 @@ def tile_multiheadattention_pa_kernel(
     nc = tc.nc
     with ExitStack() as ctx:
         const = ctx.enter_context(tc.tile_pool(name="const", bufs=1))
-        work = ctx.enter_context(tc.tile_pool(name="work", bufs=5))
+        work = ctx.enter_context(tc.tile_pool(name="work", bufs=8))
         small = ctx.enter_context(tc.tile_pool(name="small", bufs=8))
         psum = ctx.enter_context(tc.psum_pool(name="psum", bufs=8))
         ctx.enter_context(tc.manual_schedule())
@@ -77,21 +75,40 @@ def tile_multiheadattention_pa_kernel(
         w_planes = [
             const.tile([P, PASSES, N_TILE * (n1 - n0)], U8, name="w_planes%d" % n0, align_bytes=64) for n0, n1 in W_CHUNKS
         ]
+        eps = const.tile([P, 1], F32, name="eps")
+        gain_rows = const.tile([P, 256], BF16, name="gain_rows")
+        ones = const.tile([P, 256], BF16, name="ones")
+        cos_sb = const.tile([P, POS_TILES, HALF], BF16, name="cos_sb")
+        sin_sb = const.tile([P, POS_TILES, HALF], BF16, name="sin_sb")
 
         def load_codes(dst, src, c0, c1):
             nc.sync.dma_start(
                 out=dst[:].bitcast(I32), in_=src[:, :, 2 * c0 : 2 * c1].rearrange("g p c -> p g c").bitcast(I32)
             )
 
-        def load_planes(dst, src, c0, c1):
-            for quad in range(4):
-                nc.sync.dma_start(
-                    out=dst[32 * quad : 32 * quad + 4, :, :].bitcast(I32),
-                    in_=src[:, 4 * quad : 4 * quad + 4, c0:c1].rearrange("g r c -> r g c").bitcast(I32),
-                )
+        def load_plane(dst, src, c0, c1, quad):
+            nc.sync.dma_start(
+                out=dst[32 * quad : 32 * quad + 4, :, :].bitcast(I32),
+                in_=src[:, 4 * quad : 4 * quad + 4, c0:c1].rearrange("g r c -> r g c").bitcast(I32),
+            )
 
-        eps = const.tile([P, 1], F32, name="eps")
+        def load_x(i, what):
+            m0, m1 = X_CHUNKS[i]
+            if what == "codes":
+                load_codes(x_codes[i], q_input_words, P * m0, P * m1)
+            else:
+                load_plane(x_planes[i], q_input_scales, P * m0, P * m1, what)
+
+        def load_w(i, what):
+            n0, n1 = W_CHUNKS[i]
+            if what == "codes":
+                load_codes(w_codes[i], Wq_words, N_TILE * n0, N_TILE * n1)
+            else:
+                load_plane(w_planes[i], Wq_scales, N_TILE * n0, N_TILE * n1, what)
+
         nc.vector.memset(x_planes[0][:].bitcast(I32), 0)
+        nc.vector.memset(gain_rows[:], 0.0)
+        nc.vector.memset(ones[:], 1.0)
         nc.vector.memset(w_planes[0][:].bitcast(I32), 0)
         nc.vector.memset(eps[:], EPS)
         for i in range(1, len(X_CHUNKS)):
@@ -99,39 +116,23 @@ def tile_multiheadattention_pa_kernel(
         for i in range(1, len(W_CHUNKS)):
             nc.vector.memset(w_planes[i][:].bitcast(I32), 0)
 
-        gain_rows = const.tile([P, 256], BF16, name="gain_rows")
-        ones = const.tile([P, 256], BF16, name="ones")
-        cos_sb = const.tile([P, POS_TILES, HALF], BF16, name="cos_sb")
-        sin_sb = const.tile([P, POS_TILES, HALF], BF16, name="sin_sb")
-        nc.gpsimd.memset(ones[:], 1.0)
-        nc.gpsimd.memset(gain_rows[:], 0.0)
-        nc.gpsimd.dma_start(out=gain_rows[0:1, 0:HEAD], in_=q_scale.unsqueeze(0))
-        nc.gpsimd.dma_start(out=cos_sb[:], in_=cos.rearrange("(t p) j -> p t j", p=P))
-        nc.gpsimd.dma_start(out=sin_sb[:], in_=sin.rearrange("(t p) j -> p t j", p=P))
-
-        def load_x(i, what):
-            m0, m1 = X_CHUNKS[i]
-            if what == "codes":
-                load_codes(x_codes[i], q_input_words, P * m0, P * m1)
-            else:
-                load_planes(x_planes[i], q_input_scales, P * m0, P * m1)
-
-        def load_w(i, what):
-            n0, n1 = W_CHUNKS[i]
-            if what == "codes":
-                load_codes(w_codes[i], Wq_words, N_TILE * n0, N_TILE * n1)
-            else:
-                load_planes(w_planes[i], Wq_scales, N_TILE * n0, N_TILE * n1)
-
+        nc.scalar.dma_start(out=gain_rows[0:1, 0:HEAD], in_=q_scale.unsqueeze(0))
+        nc.scalar.dma_start(out=cos_sb[:], in_=cos.rearrange("(t p) j -> p t j", p=P))
+        nc.scalar.dma_start(out=sin_sb[:], in_=sin.rearrange("(t p) j -> p t j", p=P))
         load_x(0, "codes")
+        load_x(0, 0)
         load_w(0, "codes")
-        load_x(0, "planes")
-        load_w(0, "planes")
+        for quad in range(1, 4):
+            load_x(0, quad)
+        for quad in range(4):
+            load_w(0, quad)
         for i in range(1, len(X_CHUNKS)):
-            load_x(i, "planes")
+            for quad in range(4):
+                load_x(i, quad)
             load_x(i, "codes")
         for i in range(1, len(W_CHUNKS)):
-            load_w(i, "planes")
+            for quad in range(4):
+                load_w(i, quad)
             load_w(i, "codes")
 
         warm_act = const.tile([P, 1], F32, name="warm_act")
@@ -178,69 +179,117 @@ def tile_multiheadattention_pa_kernel(
                     return w_codes[i][:, g, 2 * c0 : 2 * c1], w_planes[i][:, g, c0:c1]
             raise ValueError("no chunk")
 
-        def add_and_store(engine, group, prod, res):
-            off = sum(nh for n, m, h0, nh in group)
+        def project(unit):
+            n, m, h0, nh = unit["where"]
+            acc = psum.tile([P, N_TILE], F32, tag="acc", name="acc")
+            unit["acc"] = acc
+            for g in range(PASSES):
+                xc, xp = x_operand(m, g)
+                wc, wp = w_operand(n, g, h0, nh)
+                nc.tensor.matmul_mx(
+                    out=acc[:, 0 : HEAD * nh],
+                    lhsT=xc.bitcast(FP4X4),
+                    lhsT_scale=xp,
+                    rhs=wc.bitcast(FP4X4),
+                    rhs_scale=wp,
+                    start=(g == 0),
+                    stop=(g == PASSES - 1),
+                )
+            ss = small.tile([P, BANK_HEADS], F32, name="ss")
+            rstd = small.tile([P, BANK_HEADS], F32, name="rstd")
+            unit["ss"] = ss
+            unit["rstd"] = rstd
+
+        def squares(unit, h_from, h_to):
+            for h in range(h_from, h_to):
+                junk = small.tile([P, HEAD], F32, name="junk")
+                nc.scalar.activation(
+                    out=junk[:],
+                    in_=unit["acc"][:, HEAD * h : HEAD * (h + 1)],
+                    func=ACT.Square,
+                    accum_out=unit["ss"][:, h : h + 1],
+                )
+
+        def add_and_store(engine, group):
+            heads = sum(u["where"][3] for u in group["units"])
+            prod = group["prod"]
+            res = group["res"]
             engine.tensor_tensor(
-                out=res[:, 0:off, :].rearrange("p h (two j) -> p h two j", two=2),
-                in0=prod[:, 0:off, 0, :, :],
-                in1=prod[:, 0:off, 1, ::-1, :],
+                out=res[:, 0:heads, :].rearrange("p h (two j) -> p h two j", two=2),
+                in0=prod[:, 0:heads, 0, :, :],
+                in1=prod[:, 0:heads, 1, ::-1, :],
                 op=ALU.add,
             )
-            off = 0
-            for n, m, h0, nh in group:
-                b, pt = divmod(m, POS_TILES)
-                head0 = BANK_HEADS * n + h0
-                nc.sync.dma_start(
-                    out=out[b, head0 : head0 + nh, P * pt : P * (pt + 1), :].rearrange("h p d -> p h d"),
-                    in_=res[:, off : off + nh, :],
-                )
-                off += nh
+            units = group["units"]
+            n, m, h0, nh = units[0]["where"]
+            b, pt = divmod(m, POS_TILES)
+            if STORE_BY_HEAD and len(units) > 1:
+                for h in range(BANK_HEADS):
+                    nc.sync.dma_start(
+                        out=out[b, BANK_HEADS * n + h, P * pt : P * (pt + len(units)), :].rearrange(
+                            "(u p) d -> p u d", p=P
+                        ),
+                        in_=res[:, 0:heads, :].rearrange("p (u h) d -> p u h d", h=BANK_HEADS)[:, :, h, :],
+                    )
+            else:
+                for u in units:
+                    n, m, h0, nh = u["where"]
+                    b, pt = divmod(m, POS_TILES)
+                    head0 = BANK_HEADS * n + h0
+                    nc.sync.dma_start(
+                        out=out[b, head0 : head0 + nh, P * pt : P * (pt + 1), :].rearrange("h p d -> p h d"),
+                        in_=res[:, u["off"] : u["off"] + nh, :],
+                    )
 
-        groups = make_groups()
         late = []
-        for gi, group in enumerate(groups):
+
+        def finish(unit):
+            n, m, h0, nh = unit["where"]
+            group = unit["group"]
+            pt = m % POS_TILES
+            nc.scalar.activation(
+                out=unit["rstd"][:, 0:nh], in_=unit["ss"][:, 0:nh], func=ACT.Abs_reciprocal_sqrt,
+                scale=1.0 / HEAD, bias=eps[:, 0:1],
+            )
+            for h in range(nh):
+                nc.vector.scalar_tensor_tensor(
+                    out=group["prod"][:, unit["off"] + h, :, :, :].rearrange("p e two j -> p e (two j)"),
+                    in0=unit["acc"][:, HEAD * h : HEAD * (h + 1)].unsqueeze(1).to_broadcast([P, 2, HEAD]),
+                    scalar=unit["rstd"][:, h : h + 1],
+                    in1=table[:, pt, :, :, :].rearrange("p e two j -> p e (two j)"),
+                    op0=ALU.mult,
+                    op1=ALU.mult,
+                )
+            if unit is group["units"][-1]:
+                if group["on_vector"]:
+                    late.append(group)
+                else:
+                    add_and_store(nc.gpsimd, group)
+
+        plan = make_groups()
+        pending = []
+        for gi, members in enumerate(plan):
             prod = work.tile([P, GROUP_HEADS, 2, 2, HALF], F32, name="prod")
             res = work.tile([P, GROUP_HEADS, HEAD], F32, name="res")
+            group = {"prod": prod, "res": res, "units": [], "on_vector": gi >= len(plan) - V_GROUPS}
             off = 0
-            for n, m, h0, nh in group:
-                pt = m % POS_TILES
-                width = HEAD * nh
-                acc = psum.tile([P, N_TILE], F32, tag="acc", name="acc")
-                for g in range(PASSES):
-                    xc, xp = x_operand(m, g)
-                    wc, wp = w_operand(n, g, h0, nh)
-                    nc.tensor.matmul_mx(
-                        out=acc[:, 0:width],
-                        lhsT=xc.bitcast(FP4X4),
-                        lhsT_scale=xp,
-                        rhs=wc.bitcast(FP4X4),
-                        rhs_scale=wp,
-                        start=(g == 0),
-                        stop=(g == PASSES - 1),
-                    )
-                ss = small.tile([P, BANK_HEADS], F32, name="ss")
-                rstd = small.tile([P, BANK_HEADS], F32, name="rstd")
-                for h in range(nh):
-                    junk = small.tile([P, HEAD], F32, name="junk")
-                    nc.scalar.activation(
-                        out=junk[:], in_=acc[:, HEAD * h : HEAD * (h + 1)], func=ACT.Square, accum_out=ss[:, h : h + 1]
-                    )
-                nc.scalar.activation(
-                    out=rstd[:, 0:nh], in_=ss[:, 0:nh], func=ACT.Abs_reciprocal_sqrt, scale=1.0 / HEAD, bias=eps[:, 0:1]
-                )
-                for h in range(nh):
-                    nc.vector.scalar_tensor_tensor(
-                        out=prod[:, off + h, :, :, :].rearrange("p e two j -> p e (two j)"),
-                        in0=acc[:, HEAD * h : HEAD * (h + 1)].unsqueeze(1).to_broadcast([P, 2, HEAD]),
-                        scalar=rstd[:, h : h + 1],
-                        in1=table[:, pt, :, :, :].rearrange("p e two j -> p e (two j)"),
-                        op0=ALU.mult,
-                        op1=ALU.mult,
-                    )
-                off += nh
-            if gi < len(groups) - V_GROUPS:
-                add_and_store(nc.gpsimd, group, prod, res)
-            else:
-                late.append((group, prod, res))
-        for group, prod, res in late:
-            add_and_store(nc.vector, group, prod, res)
+            for where in members:
+                group["units"].append({"where": where, "group": group, "off": off})
+                off += where[3]
+            for unit in group["units"]:
+                nh = unit["where"][3]
+                project(unit)
+                first = min(LAG_SQUARES, nh) if nh == BANK_HEADS else 0
+                squares(unit, 0, first)
+                for waiting in pending:
+                    finish(waiting)
+                pending.clear()
+                squares(unit, first, nh)
+                if nh == BANK_HEADS and LAG_SQUARES > 0:
+                    pending.append(unit)
+                else:
+                    finish(unit)
+        for waiting in pending:
+            finish(waiting)
+        for group in late:
+            add_and_store(nc.vector, group)

@@ -25,12 +25,12 @@ EPS = 1e-6
 WARM_A = 2
 WARM_B = 14
 GROUP_HEADS = 12
-V_GROUPS = 5
+V_GROUPS = 6
 W_CHUNKS = [(0, 1), (1, 4)]
 X_CHUNKS = [(0, 2), (2, 8)]
 HEAD_SPLIT = [(0, 1), (1, 1), (2, 2)]
 TAIL_SPLIT = [(0, 2), (2, 1), (3, 1)]
-MIDDLE_SIZES = [1, 2, 3, 3, 3, 3, 3, 3, 3, 2, 2, 1, 1]
+MIDDLE_SIZES = [1, 2, 3, 3, 3, 3, 3, 3, 2, 2, 1, 1, 1, 1, 1]
 LAG_SQUARES = 2
 STORE_BY_HEAD = False
 

@@ -23,11 +23,11 @@ TOKEN_TILES = 8
 COL_BLOCKS = 4
 EPS = 1e-6
 WARM_A = 2
-WARM_B = 14
+WARM_B = 20
 GROUP_HEADS = 12
 V_GROUPS = 6
 W_CHUNKS = [(0, 1), (1, 4)]
-X_CHUNKS = [(0, 2), (2, 8)]
+X_CHUNKS = [(0, 3), (3, 8)]
 HEAD_SPLIT = [(0, 1), (1, 1), (2, 2)]
 TAIL_SPLIT = [(0, 2), (2, 1), (3, 1)]
 MIDDLE_SIZES = [1, 2, 3, 3, 3, 3, 3, 3, 2, 2, 1, 1, 1, 1, 1]
@@ -106,26 +106,27 @@ def tile_multiheadattention_pa_kernel(
             else:
                 load_plane(w_planes[i], Wq_scales, N_TILE * n0, N_TILE * n1, what)
 
-        nc.vector.memset(x_planes[0][:].bitcast(I32), 0)
         nc.vector.memset(gain_rows[:], 0.0)
-        nc.vector.memset(ones[:], 1.0)
+        nc.vector.memset(x_planes[0][:].bitcast(I32), 0)
         nc.vector.memset(w_planes[0][:].bitcast(I32), 0)
+        nc.vector.memset(ones[:], 1.0)
         nc.vector.memset(eps[:], EPS)
         for i in range(1, len(X_CHUNKS)):
             nc.vector.memset(x_planes[i][:].bitcast(I32), 0)
         for i in range(1, len(W_CHUNKS)):
             nc.vector.memset(w_planes[i][:].bitcast(I32), 0)
 
+        warm_act = const.tile([P, 1], F32, name="warm_act")
         nc.scalar.dma_start(out=gain_rows[0:1, 0:HEAD], in_=q_scale.unsqueeze(0))
-        nc.scalar.dma_start(out=cos_sb[:], in_=cos.rearrange("(t p) j -> p t j", p=P))
-        nc.scalar.dma_start(out=sin_sb[:], in_=sin.rearrange("(t p) j -> p t j", p=P))
+        nc.scalar.activation(out=warm_act[:], in_=eps[:], func=ACT.Abs_reciprocal_sqrt)
         load_x(0, "codes")
-        load_x(0, 0)
         load_w(0, "codes")
-        for quad in range(1, 4):
+        for quad in range(4):
             load_x(0, quad)
         for quad in range(4):
             load_w(0, quad)
+        nc.scalar.dma_start(out=cos_sb[:], in_=cos.rearrange("(t p) j -> p t j", p=P))
+        nc.scalar.dma_start(out=sin_sb[:], in_=sin.rearrange("(t p) j -> p t j", p=P))
         for i in range(1, len(X_CHUNKS)):
             for quad in range(4):
                 load_x(i, quad)
@@ -134,9 +135,6 @@ def tile_multiheadattention_pa_kernel(
             for quad in range(4):
                 load_w(i, quad)
             load_w(i, "codes")
-
-        warm_act = const.tile([P, 1], F32, name="warm_act")
-        nc.scalar.activation(out=warm_act[:], in_=eps[:], func=ACT.Abs_reciprocal_sqrt)
 
         warm_ps = psum.tile([P, N_TILE], F32, tag="acc", name="warm_ps")
         for i in range(WARM_A):

from contextlib import ExitStack

import concourse.mybir as mybir

FLOPS = 2 * 1024 * 2048 * 2048

F32 = mybir.dt.float32
BF16 = mybir.dt.bfloat16
U8 = mybir.dt.uint8
I32 = mybir.dt.int32
FP4X4 = mybir.dt.float4_e2m1fn_x4
ALU = mybir.AluOpType
ACT = mybir.ActivationFunctionType

P = 128
PASSES = 4
HEAD = 128
HALF = 64
N_TILE = 512
BANK_HEADS = 4
POS_TILES = 4
TOKEN_TILES = 8
COL_BLOCKS = 4
EPS = 1e-6
WARM_A = 2
WARM_B = 20
GROUP_HEADS = 12
V_GROUPS = 6
W_CHUNKS = [(0, 1), (1, 4)]
X_CHUNKS = [(0, 3), (3, 8)]
HEAD_SPLIT = [(0, 1), (1, 1), (2, 2)]
TAIL_SPLIT = [(0, 2), (2, 1), (3, 1)]
MIDDLE_SIZES = [1, 2, 3, 3, 3, 3, 3, 3, 2, 2, 1, 1, 1, 1, 1]
LAG_SQUARES = 2
STORE_BY_HEAD = False


def make_groups():
    banks = [(n, m) for n in range(COL_BLOCKS) for m in range(TOKEN_TILES)]
    groups = []
    n, m = banks[0]
    for h0, nh in HEAD_SPLIT:
        groups.append([(n, m, h0, nh)])
    at = 1
    for size in MIDDLE_SIZES:
        groups.append([(n, m, 0, BANK_HEADS) for n, m in banks[at : at + size]])
        at += size
    assert at == len(banks) - 1
    n, m = banks[-1]
    for h0, nh in TAIL_SPLIT:
        groups.append([(n, m, h0, nh)])
    return groups


def tile_multiheadattention_pa_kernel(
    tc, q_input_words, q_input_scales, Wq_words, Wq_scales, q_scale, cos, sin, out
):
    nc = tc.nc
    with ExitStack() as ctx:
        const = ctx.enter_context(tc.tile_pool(name="const", bufs=1))
        work = ctx.enter_context(tc.tile_pool(name="work", bufs=8))
        small = ctx.enter_context(tc.tile_pool(name="small", bufs=8))
        psum = ctx.enter_context(tc.psum_pool(name="psum", bufs=8))
        ctx.enter_context(tc.manual_schedule())

        x_codes = [
            const.tile([P, PASSES, 256 * (m1 - m0)], U8, name="x_codes%d" % m0, align_bytes=64) for m0, m1 in X_CHUNKS
        ]
        x_planes = [
            const.tile([P, PASSES, P * (m1 - m0)], U8, name="x_planes%d" % m0, align_bytes=64) for m0, m1 in X_CHUNKS
        ]
        w_codes = [
            const.tile([P, PASSES, 2 * N_TILE * (n1 - n0)], U8, name="w_codes%d" % n0, align_bytes=64) for n0, n1 in W_CHUNKS
        ]
        w_planes = [
            const.tile([P, PASSES, N_TILE * (n1 - n0)], U8, name="w_planes%d" % n0, align_bytes=64) for n0, n1 in W_CHUNKS
        ]
        eps = const.tile([P, 1], F32, name="eps")
        gain_rows = const.tile([P, 256], BF16, name="gain_rows")
        ones = const.tile([P, 256], BF16, name="ones")
        cos_sb = const.tile([P, POS_TILES, HALF], BF16, name="cos_sb")
        sin_sb = const.tile([P, POS_TILES, HALF], BF16, name="sin_sb")

        def load_codes(dst, src, c0, c1):
            nc.sync.dma_start(
                out=dst[:].bitcast(I32), in_=src[:, :, 2 * c0 : 2 * c1].rearrange("g p c -> p g c").bitcast(I32)
            )

        def load_plane(dst, src, c0, c1, quad):
            nc.sync.dma_start(
                out=dst[32 * quad : 32 * quad + 4, :, :].bitcast(I32),
                in_=src[:, 4 * quad : 4 * quad + 4, c0:c1].rearrange("g r c -> r g c").bitcast(I32),
            )

        def load_x(i, what):
            m0, m1 = X_CHUNKS[i]
            if what == "codes":
                load_codes(x_codes[i], q_input_words, P * m0, P * m1)
            else:
                load_plane(x_planes[i], q_input_scales, P * m0, P * m1, what)

        def load_w(i, what):
            n0, n1 = W_CHUNKS[i]
            if what == "codes":
                load_codes(w_codes[i], Wq_words, N_TILE * n0, N_TILE * n1)
            else:
                load_plane(w_planes[i], Wq_scales, N_TILE * n0, N_TILE * n1, what)

        nc.vector.memset(gain_rows[:], 0.0)
        nc.vector.memset(x_planes[0][:].bitcast(I32), 0)
        nc.vector.memset(w_planes[0][:].bitcast(I32), 0)
        nc.vector.memset(ones[:], 1.0)
        nc.vector.memset(eps[:], EPS)
        for i in range(1, len(X_CHUNKS)):
            nc.vector.memset(x_planes[i][:].bitcast(I32), 0)
        for i in range(1, len(W_CHUNKS)):
            nc.vector.memset(w_planes[i][:].bitcast(I32), 0)

        warm_act = const.tile([P, 1], F32, name="warm_act")
        nc.scalar.dma_start(out=gain_rows[0:1, 0:HEAD], in_=q_scale.unsqueeze(0))
        nc.scalar.activation(out=warm_act[:], in_=eps[:], func=ACT.Abs_reciprocal_sqrt)
        load_x(0, "codes")
        load_w(0, "codes")
        for quad in range(4):
            load_x(0, quad)
        for quad in range(4):
            load_w(0, quad)
        nc.scalar.dma_start(out=cos_sb[:], in_=cos.rearrange("(t p) j -> p t j", p=P))
        nc.scalar.dma_start(out=sin_sb[:], in_=sin.rearrange("(t p) j -> p t j", p=P))
        for i in range(1, len(X_CHUNKS)):
            for quad in range(4):
                load_x(i, quad)
            load_x(i, "codes")
        for i in range(1, len(W_CHUNKS)):
            for quad in range(4):
                load_w(i, quad)
            load_w(i, "codes")

        warm_ps = psum.tile([P, N_TILE], F32, tag="acc", name="warm_ps")
        for i in range(WARM_A):
            nc.tensor.matmul(out=warm_ps[:, 0:256], lhsT=ones[:, 0:P], rhs=ones[:], start=True, stop=True)
        gain_ps = psum.tile([P, N_TILE], F32, tag="acc", name="gain_ps")
        nc.tensor.matmul(out=gain_ps[:, 0:256], lhsT=ones[:, 0:P], rhs=gain_rows[:], start=True, stop=True)
        for i in range(WARM_B):
            nc.tensor.matmul(out=warm_ps[:, 0:256], lhsT=ones[:, 0:P], rhs=ones[:], start=True, stop=True)

        gain = const.tile([P, 2, HALF], F32, name="gain")
        gain_pm = const.tile([P, 2, HALF], F32, name="gain_pm")
        table = const.tile([P, POS_TILES, 2, 2, HALF], F32, name="table")
        nc.vector.tensor_scalar_add(
            out=gain[:].rearrange("p two j -> p (two j)"), in0=gain_ps[:, 0:HEAD], scalar1=1.0
        )
        nc.vector.tensor_scalar_add(out=gain_pm[:, 0, :], in0=gain_ps[:, 0:HALF], scalar1=1.0)
        nc.vector.tensor_scalar(
            out=gain_pm[:, 1, :], in0=gain_ps[:, HALF:HEAD], scalar1=-1.0, scalar2=-1.0, op0=ALU.mult, op1=ALU.add
        )
        full = [P, POS_TILES, 2, HALF]
        nc.vector.tensor_tensor(
            out=table[:, :, 0, :, :], in0=cos_sb[:].unsqueeze(2).to_broadcast(full), in1=gain[:].unsqueeze(1).to_broadcast(full), op=ALU.mult
        )
        nc.vector.tensor_tensor(
            out=table[:, :, 1, :, :], in0=sin_sb[:].unsqueeze(2).to_broadcast(full), in1=gain_pm[:].unsqueeze(1).to_broadcast(full), op=ALU.mult
        )

        def x_operand(m, g):
            for i, (m0, m1) in enumerate(X_CHUNKS):
                if m0 <= m < m1:
                    k = m - m0
                    return x_codes[i][:, g, 256 * k : 256 * (k + 1)], x_planes[i][:, g, P * k : P * (k + 1)]
            raise ValueError("no chunk")

        def w_operand(n, g, h0, nh):
            for i, (n0, n1) in enumerate(W_CHUNKS):
                if n0 <= n < n1:
                    c0 = N_TILE * (n - n0) + HEAD * h0
                    c1 = c0 + HEAD * nh
                    return w_codes[i][:, g, 2 * c0 : 2 * c1], w_planes[i][:, g, c0:c1]
            raise ValueError("no chunk")

        def project(unit):
            n, m, h0, nh = unit["where"]
            acc = psum.tile([P, N_TILE], F32, tag="acc", name="acc")
            unit["acc"] = acc
            for g in range(PASSES):
                xc, xp = x_operand(m, g)
                wc, wp = w_operand(n, g, h0, nh)
                nc.tensor.matmul_mx(
                    out=acc[:, 0 : HEAD * nh],
                    lhsT=xc.bitcast(FP4X4),
                    lhsT_scale=xp,
                    rhs=wc.bitcast(FP4X4),
                    rhs_scale=wp,
                    start=(g == 0),
                    stop=(g == PASSES - 1),
                )
            ss = small.tile([P, BANK_HEADS], F32, name="ss")
            rstd = small.tile([P, BANK_HEADS], F32, name="rstd")
            unit["ss"] = ss
            unit["rstd"] = rstd

        def squares(unit, h_from, h_to):
            for h in range(h_from, h_to):
                junk = small.tile([P, HEAD], F32, name="junk")
                nc.scalar.activation(
                    out=junk[:],
                    in_=unit["acc"][:, HEAD * h : HEAD * (h + 1)],
                    func=ACT.Square,
                    accum_out=unit["ss"][:, h : h + 1],
                )

        def add_and_store(engine, group):
            heads = sum(u["where"][3] for u in group["units"])
            prod = group["prod"]
            res = group["res"]
            engine.tensor_tensor(
                out=res[:, 0:heads, :].rearrange("p h (two j) -> p h two j", two=2),
                in0=prod[:, 0:heads, 0, :, :],
                in1=prod[:, 0:heads, 1, ::-1, :],
                op=ALU.add,
            )
            units = group["units"]
            n, m, h0, nh = units[0]["where"]
            b, pt = divmod(m, POS_TILES)
            if STORE_BY_HEAD and len(units) > 1:
                for h in range(BANK_HEADS):
                    nc.sync.dma_start(
                        out=out[b, BANK_HEADS * n + h, P * pt : P * (pt + len(units)), :].rearrange(
                            "(u p) d -> p u d", p=P
                        ),
                        in_=res[:, 0:heads, :].rearrange("p (u h) d -> p u h d", h=BANK_HEADS)[:, :, h, :],
                    )
            else:
                for u in units:
                    n, m, h0, nh = u["where"]
                    b, pt = divmod(m, POS_TILES)
                    head0 = BANK_HEADS * n + h0
                    nc.sync.dma_start(
                        out=out[b, head0 : head0 + nh, P * pt : P * (pt + 1), :].rearrange("h p d -> p h d"),
                        in_=res[:, u["off"] : u["off"] + nh, :],
                    )

        late = []

        def finish(unit):
            n, m, h0, nh = unit["where"]
            group = unit["group"]
            pt = m % POS_TILES
            nc.scalar.activation(
                out=unit["rstd"][:, 0:nh], in_=unit["ss"][:, 0:nh], func=ACT.Abs_reciprocal_sqrt,
                scale=1.0 / HEAD, bias=eps[:, 0:1],
            )
            for h in range(nh):
                nc.vector.scalar_tensor_tensor(
                    out=group["prod"][:, unit["off"] + h, :, :, :].rearrange("p e two j -> p e (two j)"),
                    in0=unit["acc"][:, HEAD * h : HEAD * (h + 1)].unsqueeze(1).to_broadcast([P, 2, HEAD]),
                    scalar=unit["rstd"][:, h : h + 1],
                    in1=table[:, pt, :, :, :].rearrange("p e two j -> p e (two j)"),
                    op0=ALU.mult,
                    op1=ALU.mult,
                )
            if unit is group["units"][-1]:
                if group["on_vector"]:
                    late.append(group)
                else:
                    add_and_store(nc.gpsimd, group)

        plan = make_groups()
        pending = []
        for gi, members in enumerate(plan):
            prod = work.tile([P, GROUP_HEADS, 2, 2, HALF], F32, name="prod")
            res = work.tile([P, GROUP_HEADS, HEAD], F32, name="res")
            group = {"prod": prod, "res": res, "units": [], "on_vector": gi >= len(plan) - V_GROUPS}
            off = 0
            for where in members:
                group["units"].append({"where": where, "group": group, "off": off})
                off += where[3]
            for unit in group["units"]:
                nh = unit["where"][3]
                project(unit)
                first = min(LAG_SQUARES, nh) if nh == BANK_HEADS else 0
                squares(unit, 0, first)
                for waiting in pending:
                    finish(waiting)
                pending.clear()
                squares(unit, first, nh)
                if nh == BANK_HEADS and LAG_SQUARES > 0:
                    pending.append(unit)
                else:
                    finish(unit)
        for waiting in pending:
            finish(waiting)
        for group in late:
            add_and_store(nc.vector, group)
